import numpy as np
import ml_dtypes


def mxq(x, axis, fmt="e4m3"):
    dtype, down = {"e4m3": (ml_dtypes.float8_e4m3fn, 7), "e5m2": (ml_dtypes.float8_e5m2, 14)}[fmt]
    v = np.moveaxis(np.asarray(x, np.float32).astype(ml_dtypes.bfloat16).astype(np.float64), axis, -1)
    blocks = v.reshape(v.shape[:-1] + (-1, 32))
    amax = np.abs(blocks).max(-1, keepdims=True)
    byte = np.maximum(np.where(amax > 0, np.frexp(amax)[1] - 1 + 127, 0) - down, 1)
    scale = np.exp2(byte - 127.0)
    codes = (blocks / scale).astype(np.float32).astype(dtype).astype(np.float64)
    return np.moveaxis((codes * scale).reshape(v.shape), -1, axis)


WIDE = False


def mx_kscale(k):
    if not WIDE:
        return np.ones(k)
    levels = np.array([10, -10, 5, -5, 0])
    a = np.random.permutation(np.resize(levels, k // 512 * 4)).reshape(k // 512, 4)
    idx = np.arange(k)
    return np.exp2(a[idx // 512, idx % 128 // 32])


BF16 = ml_dtypes.bfloat16


def bf(x):
    return np.asarray(x, np.float32).astype(BF16)


def f64(x):
    return np.asarray(x).astype(np.float64)


B, P, L, FI, FO = 128, 2, 3, 512, 512
C = (L + 1) * (L + 1)


def setup_inputs():
    s = mx_kscale(FI)
    return {"x": bf(np.random.standard_normal((B, P, C, FI)) * s),
            "W_e": bf(np.random.standard_normal((L + 1, FI, FO)) / np.sqrt(FI) / s[:, None]),
            "W_o": bf(np.random.standard_normal((L + 1, FI, FO)) / np.sqrt(FI) / s[:, None]),
            "b": bf(np.random.standard_normal(FO) * 0.5)}


def reference(x, W_e, W_o, b):
    xq = mxq(f64(x), 3, "e4m3")
    weq = mxq(f64(W_e), 1, "e4m3")
    woq = mxq(f64(W_o), 1, "e4m3")
    outs_e, outs_o = [], []
    for l in range(L + 1):
        seg = xq[:, :, l * l:(l + 1) * (l + 1), :]
        oe = seg[:, 0] @ weq[l]
        if l == 0:
            oe = oe + f64(b)
        oo = seg[:, 1] @ woq[l]
        outs_e.append(oe)
        outs_o.append(oo)
    return np.stack([np.concatenate(outs_e, axis=-2), np.concatenate(outs_o, axis=-2)], axis=-3)

@@ -1,0 +1,198 @@
+from contextlib import ExitStack
+
+import concourse.mybir as mybir
+from concourse.masks import make_identity
+
+F32 = mybir.dt.float32
+BF16 = mybir.dt.bfloat16
+U32 = mybir.dt.uint32
+U8 = mybir.dt.uint8
+FP8X4 = mybir.dt.float8_e4m3fn_x4
+
+P = 128
+F = 512
+FLOPS = 2 * 128 * 2 * 16 * 512 * 512
+
+GROUPS = [(0, 12), (0, 8), (1, 12), (1, 8), (0, 4), (0, 0), (1, 4), (1, 0)]
+WEIGHTS = [(0, 3), (0, 2), (1, 3), (1, 2), (0, 1), (0, 0), (1, 1), (1, 0)]
+DEGREE = [0, 1, 1, 1, 2, 2, 2, 2, 2, 3, 3, 3, 3, 3, 3, 3]
+
+
+def tile_dense_pa_kernel(tc, x, W_e, W_o, b, out):
+    nc = tc.nc
+    with ExitStack() as ctx:
+        keep = ctx.enter_context(tc.tile_pool(name="keep", bufs=1))
+        wgp = ctx.enter_context(tc.tile_pool(name="wgp", bufs=3))
+        xgp = ctx.enter_context(tc.tile_pool(name="xgp", bufs=3))
+        pst = ctx.enter_context(tc.psum_pool(name="pst", bufs=3))
+        pso = ctx.enter_context(tc.psum_pool(name="pso", bufs=5))
+        W = [W_e, W_o]
+
+        wraw = {}
+        xsrc = {}
+
+        def load_w1(par, deg):
+            t = keep.tile([P, 4, F], BF16, name="wr%d%d" % (par, deg))
+            nc.sync.dma_start(out=t[:], in_=W[par][deg].rearrange("(p t) f -> p t f", t=4))
+            wraw[(par, deg)] = t[:]
+
+        def load_w01(par):
+            t = keep.tile([P, 2, 4, F], BF16, name="wr%d01" % par)
+            nc.sync.dma_start(out=t[:], in_=W[par][0:2].rearrange("l (p t) f -> p l t f", t=4))
+            wraw[(par, 0)] = t[:, 0]
+            wraw[(par, 1)] = t[:, 1]
+
+        def load_x(par, c0, n):
+            t = keep.tile([P, n * F], BF16, name="x%d_%d" % (par, c0))
+            nc.sync.dma_start(out=t[:], in_=x[:, par, c0:c0 + n, :].rearrange("n c f -> n (c f)"))
+            words = t[:].bitcast(F32)
+            for q in range(n // 4):
+                xsrc[(par, c0 + 4 * q)] = words[:, q * 4 * (F // 2):(q + 1) * 4 * (F // 2)]
+
+        load_w1(0, 3)
+        load_x(0, 12, 4)
+        load_x(0, 8, 4)
+        load_w1(0, 2)
+        load_x(1, 8, 8)
+        load_w1(1, 3)
+        load_w1(1, 2)
+        load_x(0, 0, 8)
+        load_w01(0)
+        load_x(1, 0, 8)
+        load_w01(1)
+
+        ident = keep.tile([P, P], F32, name="ident")
+        make_identity(nc, ident[:])
+        brow = keep.tile([P, F], BF16, name="brow")
+        nc.vector.memset(brow[:], 0.0)
+        nc.scalar.dma_start(out=brow[0:1, :], in_=b.rearrange("(o f) -> o f", o=1))
+        ones = keep.tile([P, P], BF16, name="ones")
+        nc.vector.memset(ones[:], 1.0)
+        bias_sb = keep.tile([P, F], F32, name="bias_sb")
+
+        outs = {}
+        for (par, c0, n) in [(0, 8, 8), (1, 8, 8), (0, 0, 8), (1, 4, 4), (1, 0, 4)]:
+            t = keep.tile([P, n * F], F32, name="o%d_%d" % (par, c0))
+            for q in range(n // 4):
+                outs[(par, c0 + 4 * q)] = (t, q * 4 * F)
+
+        wgrp = {}
+        wcod = {}
+        wsca = {}
+        xtb = {}
+        xgrp = {}
+        xcod = {}
+        xsca = {}
+
+        def w_regroup(i):
+            g = wgp.tile([P, F, 4], BF16, align_bytes=64, tag="wg", name="wg%d" % i)
+            nc.vector.tensor_copy(
+                out=g[:].rearrange("p (c i) t -> p c t i", i=4),
+                in_=wraw[WEIGHTS[i]].rearrange("p t (c i) -> p c t i", i=4),
+            )
+            wgrp[i] = g
+
+        def w_quant(i):
+            c = keep.tile([P, F], U32, align_bytes=64, name="wc%d" % i)
+            s = keep.tile([P, F], U8, align_bytes=64, name="ws%d" % i)
+            nc.vector.quantize_mx(
+                out=c[:].bitcast(FP8X4), scales=s[:], in_=wgrp[i][:].rearrange("p w t -> p (w t)")
+            )
+            wcod[WEIGHTS[i]] = c
+            wsca[WEIGHTS[i]] = s
+
+        def x_transpose(g):
+            src = xsrc[GROUPS[g]]
+            banks = []
+            for h in range(2):
+                bank = pst.tile([P, 4, P], F32, tag="xt", name="xt%d_%d" % (g, h))
+                for j in range(2):
+                    base = (2 * h + j) * (F // 2)
+                    for u in range(2):
+                        nc.tensor.transpose(
+                            out=bank[:, 2 * j + u, :],
+                            in_=src[:, base + u:base + F // 2:2],
+                            identity=ident[:],
+                        )
+                banks.append(bank)
+            xtb[g] = banks
+
+        def x_copy(g):
+            t = xgp.tile([P, 4 * F], BF16, align_bytes=64, tag="xg", name="xg%d" % g)
+            words = t[:].bitcast(F32)
+            for h in range(2):
+                dst = words[:, h * F:(h + 1) * F].rearrange("p (j n u) -> p j n u", j=2, u=2)
+                src = xtb[g][h][:].rearrange("p (j u) n -> p j n u", u=2)
+                if h == 0:
+                    nc.scalar.copy(out=dst, in_=src)
+                else:
+                    nc.vector.tensor_copy(out=dst, in_=src)
+            xgrp[g] = t
+
+        def x_quant(g):
+            c = keep.tile([P, 4 * P], U32, align_bytes=64, name="xc%d" % g)
+            s = keep.tile([P, 4 * P], U8, align_bytes=64, name="xs%d" % g)
+            nc.vector.quantize_mx(out=c[:].bitcast(FP8X4), scales=s[:], in_=xgrp[g][:])
+            xcod[g] = c
+            xsca[g] = s
+
+        def product(g, vector_share):
+            par, c0 = GROUPS[g]
+            order = sorted(range(4), key=lambda j: -DEGREE[c0 + j])
+            ot, off = outs[GROUPS[g]]
+            for n, j in enumerate(order):
+                key = (par, DEGREE[c0 + j])
+                acc = pso.tile([P, F], F32, tag="acc", name="acc%d_%d" % (g, j))
+                nc.tensor.matmul_mx(
+                    out=acc[:],
+                    lhsT=xcod[g][:, j * P:(j + 1) * P].bitcast(FP8X4),
+                    lhsT_scale=xsca[g][:, j * P:(j + 1) * P],
+                    rhs=wcod[key][:].bitcast(FP8X4),
+                    rhs_scale=wsca[key][:],
+                    start=True,
+                    stop=True,
+                )
+                dst = ot[:, off + j * F:off + (j + 1) * F]
+                if par == 0 and c0 + j == 0:
+                    nc.vector.tensor_tensor(out=dst, in0=acc[:], in1=bias_sb[:], op=mybir.AluOpType.add)
+                elif n in vector_share:
+                    nc.vector.tensor_copy(out=dst, in_=acc[:])
+                else:
+                    nc.scalar.copy(out=dst, in_=acc[:])
+
+        def store(par, c0, n):
+            ot, off = outs[(par, c0)]
+            nc.sync.dma_start(
+                out=out[:, par, c0:c0 + n, :].rearrange("n c f -> n (c f)"), in_=ot[:, off:off + n * F]
+            )
+
+        w_regroup(0)
+        w_quant(0)
+        x_transpose(0)
+        x_transpose(1)
+        x_copy(0)
+        x_quant(0)
+        for g in range(8):
+            if g + 1 < 8:
+                x_copy(g + 1)
+                w_regroup(g + 1)
+            product(g, (1, 3) if g == 7 else ())
+            if g == 2:
+                bias_ps = pso.tile([P, F], F32, tag="acc", name="bias_ps")
+                nc.tensor.matmul(out=bias_ps[:], lhsT=ones[:], rhs=brow[:], start=True, stop=True)
+                nc.scalar.copy(out=bias_sb[:], in_=bias_ps[:])
+            if g + 2 < 8:
+                x_transpose(g + 2)
+            if g + 1 < 8:
+                x_quant(g + 1)
+                w_quant(g + 1)
+            if g == 1:
+                store(0, 8, 8)
+            elif g == 3:
+                store(1, 8, 8)
+            elif g == 5:
+                store(0, 0, 8)
+            elif g == 6:
+                store(1, 4, 4)
+            elif g == 7:
+                store(1, 0, 4)

@@ -15,6 +15,7 @@ FLOPS = 2 * 128 * 2 * 16 * 512 * 512
 
 GROUPS = [(0, 12), (0, 8), (1, 12), (1, 8), (0, 4), (0, 0), (1, 4), (1, 0)]
 WEIGHTS = [(0, 3), (0, 2), (1, 3), (1, 2), (0, 1), (0, 0), (1, 1), (1, 0)]
+SCALAR_BOTH = (0, 3, 6)
 DEGREE = [0, 1, 1, 1, 2, 2, 2, 2, 2, 3, 3, 3, 3, 3, 3, 3]
 
 
@@ -27,6 +28,7 @@ def tile_dense_pa_kernel(tc, x, W_e, W_o, b, out):
         pst = ctx.enter_context(tc.psum_pool(name="pst", bufs=3))
         pso = ctx.enter_context(tc.psum_pool(name="pso", bufs=5))
         W = [W_e, W_o]
+        ctx.enter_context(tc.manual_schedule())
 
         wraw = {}
         xsrc = {}
@@ -71,10 +73,10 @@ def tile_dense_pa_kernel(tc, x, W_e, W_o, b, out):
         bias_sb = keep.tile([P, F], F32, name="bias_sb")
 
         outs = {}
-        for (par, c0, n) in [(0, 8, 8), (1, 8, 8), (0, 0, 8), (1, 4, 4), (1, 0, 4)]:
+        for (par, c0, n) in [(0, 8, 8), (1, 8, 8), (0, 4, 4), (0, 0, 4), (1, 4, 4), (1, 2, 2), (1, 0, 2)]:
             t = keep.tile([P, n * F], F32, name="o%d_%d" % (par, c0))
-            for q in range(n // 4):
-                outs[(par, c0 + 4 * q)] = (t, q * 4 * F)
+            for q in range(n):
+                outs[(par, c0 + q)] = (t, q * F)
 
         wgrp = {}
         wcod = {}
@@ -123,7 +125,7 @@ def tile_dense_pa_kernel(tc, x, W_e, W_o, b, out):
             for h in range(2):
                 dst = words[:, h * F:(h + 1) * F].rearrange("p (j n u) -> p j n u", j=2, u=2)
                 src = xtb[g][h][:].rearrange("p (j u) n -> p j n u", u=2)
-                if h == 0:
+                if h == 0 or g in SCALAR_BOTH:
                     nc.scalar.copy(out=dst, in_=src)
                 else:
                     nc.vector.tensor_copy(out=dst, in_=src)
@@ -138,9 +140,9 @@ def tile_dense_pa_kernel(tc, x, W_e, W_o, b, out):
 
         def product(g, vector_share):
             par, c0 = GROUPS[g]
-            order = sorted(range(4), key=lambda j: -DEGREE[c0 + j])
-            ot, off = outs[GROUPS[g]]
+            order = sorted(range(4), key=lambda j: (-DEGREE[c0 + j], -j))
             for n, j in enumerate(order):
+                ot, off = outs[(par, c0 + j)]
                 key = (par, DEGREE[c0 + j])
                 acc = pso.tile([P, F], F32, tag="acc", name="acc%d_%d" % (g, j))
                 nc.tensor.matmul_mx(
@@ -152,7 +154,7 @@ def tile_dense_pa_kernel(tc, x, W_e, W_o, b, out):
                     start=True,
                     stop=True,
                 )
-                dst = ot[:, off + j * F:off + (j + 1) * F]
+                dst = ot[:, off:off + F]
                 if par == 0 and c0 + j == 0:
                     nc.vector.tensor_tensor(out=dst, in0=acc[:], in1=bias_sb[:], op=mybir.AluOpType.add)
                 elif n in vector_share:
@@ -167,10 +169,10 @@ def tile_dense_pa_kernel(tc, x, W_e, W_o, b, out):
             )
 
         w_regroup(0)
-        w_quant(0)
         x_transpose(0)
-        x_transpose(1)
         x_copy(0)
+        w_quant(0)
+        x_transpose(1)
         x_quant(0)
         for g in range(8):
             if g + 1 < 8:
@@ -190,9 +192,12 @@ def tile_dense_pa_kernel(tc, x, W_e, W_o, b, out):
                 store(0, 8, 8)
             elif g == 3:
                 store(1, 8, 8)
+            elif g == 4:
+                store(0, 4, 4)
             elif g == 5:
-                store(0, 0, 8)
+                store(0, 0, 4)
             elif g == 6:
                 store(1, 4, 4)
             elif g == 7:
-                store(1, 0, 4)
+                store(1, 2, 2)
+                store(1, 0, 2)

@@ -73,7 +73,7 @@ def tile_dense_pa_kernel(tc, x, W_e, W_o, b, out):
         bias_sb = keep.tile([P, F], F32, name="bias_sb")
 
         outs = {}
-        for (par, c0, n) in [(0, 8, 8), (1, 8, 8), (0, 4, 4), (0, 0, 4), (1, 4, 4), (1, 2, 2), (1, 0, 2)]:
+        for (par, c0, n) in [(0, 8, 8), (1, 8, 8), (0, 0, 8), (1, 0, 8)]:
             t = keep.tile([P, n * F], F32, name="o%d_%d" % (par, c0))
             for q in range(n):
                 outs[(par, c0 + q)] = (t, q * F)
@@ -192,12 +192,7 @@ def tile_dense_pa_kernel(tc, x, W_e, W_o, b, out):
                 store(0, 8, 8)
             elif g == 3:
                 store(1, 8, 8)
-            elif g == 4:
-                store(0, 4, 4)
             elif g == 5:
-                store(0, 0, 4)
-            elif g == 6:
-                store(1, 4, 4)
+                store(0, 0, 8)
             elif g == 7:
-                store(1, 2, 2)
-                store(1, 0, 2)
+                store(1, 0, 8)

@@ -34,18 +34,18 @@ def tile_dense_pa_kernel(tc, x, W_e, W_o, b, out):
         xsrc = {}
 
         def load_w1(par, deg):
-            t = keep.tile([P, 4, F], BF16, name="wr%d%d" % (par, deg))
+            t = keep.tile([P, 4, F], BF16, align_bytes=256, name="wr%d%d" % (par, deg))
             nc.sync.dma_start(out=t[:], in_=W[par][deg].rearrange("(p t) f -> p t f", t=4))
             wraw[(par, deg)] = t[:]
 
         def load_w01(par):
-            t = keep.tile([P, 2, 4, F], BF16, name="wr%d01" % par)
+            t = keep.tile([P, 2, 4, F], BF16, align_bytes=256, name="wr%d01" % par)
             nc.sync.dma_start(out=t[:], in_=W[par][0:2].rearrange("l (p t) f -> p l t f", t=4))
             wraw[(par, 0)] = t[:, 0]
             wraw[(par, 1)] = t[:, 1]
 
         def load_x(par, c0, n):
-            t = keep.tile([P, n * F], BF16, name="x%d_%d" % (par, c0))
+            t = keep.tile([P, n * F], BF16, align_bytes=256, name="x%d_%d" % (par, c0))
             nc.sync.dma_start(out=t[:], in_=x[:, par, c0:c0 + n, :].rearrange("n c f -> n (c f)"))
             words = t[:].bitcast(F32)
             for q in range(n // 4):
@@ -74,7 +74,7 @@ def tile_dense_pa_kernel(tc, x, W_e, W_o, b, out):
 
         outs = {}
         for (par, c0, n) in [(0, 8, 8), (1, 8, 8), (0, 0, 8), (1, 0, 8)]:
-            t = keep.tile([P, n * F], F32, name="o%d_%d" % (par, c0))
+            t = keep.tile([P, n * F], F32, align_bytes=256, name="o%d_%d" % (par, c0))
             for q in range(n):
                 outs[(par, c0 + q)] = (t, q * F)
 

from contextlib import ExitStack

import concourse.mybir as mybir
from concourse.masks import make_identity

F32 = mybir.dt.float32
BF16 = mybir.dt.bfloat16
U32 = mybir.dt.uint32
U8 = mybir.dt.uint8
FP8X4 = mybir.dt.float8_e4m3fn_x4

P = 128
F = 512
FLOPS = 2 * 128 * 2 * 16 * 512 * 512

GROUPS = [(0, 12), (0, 8), (1, 12), (1, 8), (0, 4), (0, 0), (1, 4), (1, 0)]
WEIGHTS = [(0, 3), (0, 2), (1, 3), (1, 2), (0, 1), (0, 0), (1, 1), (1, 0)]
SCALAR_BOTH = (0, 3, 6)
DEGREE = [0, 1, 1, 1, 2, 2, 2, 2, 2, 3, 3, 3, 3, 3, 3, 3]


def tile_dense_pa_kernel(tc, x, W_e, W_o, b, out):
    nc = tc.nc
    with ExitStack() as ctx:
        keep = ctx.enter_context(tc.tile_pool(name="keep", bufs=1))
        wgp = ctx.enter_context(tc.tile_pool(name="wgp", bufs=3))
        xgp = ctx.enter_context(tc.tile_pool(name="xgp", bufs=3))
        pst = ctx.enter_context(tc.psum_pool(name="pst", bufs=3))
        pso = ctx.enter_context(tc.psum_pool(name="pso", bufs=5))
        W = [W_e, W_o]
        ctx.enter_context(tc.manual_schedule())

        wraw = {}
        xsrc = {}

        def load_w1(par, deg):
            t = keep.tile([P, 4, F], BF16, align_bytes=256, name="wr%d%d" % (par, deg))
            nc.sync.dma_start(out=t[:], in_=W[par][deg].rearrange("(p t) f -> p t f", t=4))
            wraw[(par, deg)] = t[:]

        def load_w01(par):
            t = keep.tile([P, 2, 4, F], BF16, align_bytes=256, name="wr%d01" % par)
            nc.sync.dma_start(out=t[:], in_=W[par][0:2].rearrange("l (p t) f -> p l t f", t=4))
            wraw[(par, 0)] = t[:, 0]
            wraw[(par, 1)] = t[:, 1]

        def load_x(par, c0, n):
            t = keep.tile([P, n * F], BF16, align_bytes=256, name="x%d_%d" % (par, c0))
            nc.sync.dma_start(out=t[:], in_=x[:, par, c0:c0 + n, :].rearrange("n c f -> n (c f)"))
            words = t[:].bitcast(F32)
            for q in range(n // 4):
                xsrc[(par, c0 + 4 * q)] = words[:, q * 4 * (F // 2):(q + 1) * 4 * (F // 2)]

        load_w1(0, 3)
        load_x(0, 12, 4)
        load_x(0, 8, 4)
        load_w1(0, 2)
        load_x(1, 8, 8)
        load_w1(1, 3)
        load_w1(1, 2)
        load_x(0, 0, 8)
        load_w01(0)
        load_x(1, 0, 8)
        load_w01(1)

        ident = keep.tile([P, P], F32, name="ident")
        make_identity(nc, ident[:])
        brow = keep.tile([P, F], BF16, name="brow")
        nc.vector.memset(brow[:], 0.0)
        nc.scalar.dma_start(out=brow[0:1, :], in_=b.rearrange("(o f) -> o f", o=1))
        ones = keep.tile([P, P], BF16, name="ones")
        nc.vector.memset(ones[:], 1.0)
        bias_sb = keep.tile([P, F], F32, name="bias_sb")

        outs = {}
        for (par, c0, n) in [(0, 8, 8), (1, 8, 8), (0, 0, 8), (1, 0, 8)]:
            t = keep.tile([P, n * F], F32, align_bytes=256, name="o%d_%d" % (par, c0))
            for q in range(n):
                outs[(par, c0 + q)] = (t, q * F)

        wgrp = {}
        wcod = {}
        wsca = {}
        xtb = {}
        xgrp = {}
        xcod = {}
        xsca = {}

        def w_regroup(i):
            g = wgp.tile([P, F, 4], BF16, align_bytes=64, tag="wg", name="wg%d" % i)
            nc.vector.tensor_copy(
                out=g[:].rearrange("p (c i) t -> p c t i", i=4),
                in_=wraw[WEIGHTS[i]].rearrange("p t (c i) -> p c t i", i=4),
            )
            wgrp[i] = g

        def w_quant(i):
            c = keep.tile([P, F], U32, align_bytes=64, name="wc%d" % i)
            s = keep.tile([P, F], U8, align_bytes=64, name="ws%d" % i)
            nc.vector.quantize_mx(
                out=c[:].bitcast(FP8X4), scales=s[:], in_=wgrp[i][:].rearrange("p w t -> p (w t)")
            )
            wcod[WEIGHTS[i]] = c
            wsca[WEIGHTS[i]] = s

        def x_transpose(g):
            src = xsrc[GROUPS[g]]
            banks = []
            for h in range(2):
                bank = pst.tile([P, 4, P], F32, tag="xt", name="xt%d_%d" % (g, h))
                for j in range(2):
                    base = (2 * h + j) * (F // 2)
                    for u in range(2):
                        nc.tensor.transpose(
                            out=bank[:, 2 * j + u, :],
                            in_=src[:, base + u:base + F // 2:2],
                            identity=ident[:],
                        )
                banks.append(bank)
            xtb[g] = banks

        def x_copy(g):
            t = xgp.tile([P, 4 * F], BF16, align_bytes=64, tag="xg", name="xg%d" % g)
            words = t[:].bitcast(F32)
            for h in range(2):
                dst = words[:, h * F:(h + 1) * F].rearrange("p (j n u) -> p j n u", j=2, u=2)
                src = xtb[g][h][:].rearrange("p (j u) n -> p j n u", u=2)
                if h == 0 or g in SCALAR_BOTH:
                    nc.scalar.copy(out=dst, in_=src)
                else:
                    nc.vector.tensor_copy(out=dst, in_=src)
            xgrp[g] = t

        def x_quant(g):
            c = keep.tile([P, 4 * P], U32, align_bytes=64, name="xc%d" % g)
            s = keep.tile([P, 4 * P], U8, align_bytes=64, name="xs%d" % g)
            nc.vector.quantize_mx(out=c[:].bitcast(FP8X4), scales=s[:], in_=xgrp[g][:])
            xcod[g] = c
            xsca[g] = s

        def product(g, vector_share):
            par, c0 = GROUPS[g]
            order = sorted(range(4), key=lambda j: (-DEGREE[c0 + j], -j))
            for n, j in enumerate(order):
                ot, off = outs[(par, c0 + j)]
                key = (par, DEGREE[c0 + j])
                acc = pso.tile([P, F], F32, tag="acc", name="acc%d_%d" % (g, j))
                nc.tensor.matmul_mx(
                    out=acc[:],
                    lhsT=xcod[g][:, j * P:(j + 1) * P].bitcast(FP8X4),
                    lhsT_scale=xsca[g][:, j * P:(j + 1) * P],
                    rhs=wcod[key][:].bitcast(FP8X4),
                    rhs_scale=wsca[key][:],
                    start=True,
                    stop=True,
                )
                dst = ot[:, off:off + F]
                if par == 0 and c0 + j == 0:
                    nc.vector.tensor_tensor(out=dst, in0=acc[:], in1=bias_sb[:], op=mybir.AluOpType.add)
                elif n in vector_share:
                    nc.vector.tensor_copy(out=dst, in_=acc[:])
                else:
                    nc.scalar.copy(out=dst, in_=acc[:])

        def store(par, c0, n):
            ot, off = outs[(par, c0)]
            nc.sync.dma_start(
                out=out[:, par, c0:c0 + n, :].rearrange("n c f -> n (c f)"), in_=ot[:, off:off + n * F]
            )

        w_regroup(0)
        x_transpose(0)
        x_copy(0)
        w_quant(0)
        x_transpose(1)
        x_quant(0)
        for g in range(8):
            if g + 1 < 8:
                x_copy(g + 1)
                w_regroup(g + 1)
            product(g, (1, 3) if g == 7 else ())
            if g == 2:
                bias_ps = pso.tile([P, F], F32, tag="acc", name="bias_ps")
                nc.tensor.matmul(out=bias_ps[:], lhsT=ones[:], rhs=brow[:], start=True, stop=True)
                nc.scalar.copy(out=bias_sb[:], in_=bias_ps[:])
            if g + 2 < 8:
                x_transpose(g + 2)
            if g + 1 < 8:
                x_quant(g + 1)
                w_quant(g + 1)
            if g == 1:
                store(0, 8, 8)
            elif g == 3:
                store(1, 8, 8)
            elif g == 5:
                store(0, 0, 8)
            elif g == 7:
                store(1, 0, 8)
